import numpy as np
import ml_dtypes


def mxq(x, axis, fmt="e4m3"):
    dtype, down = {"e4m3": (ml_dtypes.float8_e4m3fn, 7), "e5m2": (ml_dtypes.float8_e5m2, 14)}[fmt]
    v = np.moveaxis(np.asarray(x, np.float32).astype(ml_dtypes.bfloat16).astype(np.float64), axis, -1)
    blocks = v.reshape(v.shape[:-1] + (-1, 32))
    amax = np.abs(blocks).max(-1, keepdims=True)
    byte = np.maximum(np.where(amax > 0, np.frexp(amax)[1] - 1 + 127, 0) - down, 1)
    scale = np.exp2(byte - 127.0)
    codes = (blocks / scale).astype(np.float32).astype(dtype).astype(np.float64)
    return np.moveaxis((codes * scale).reshape(v.shape), -1, axis)


WIDE = False


def mx_kscale(k):
    if not WIDE:
        return np.ones(k)
    levels = np.array([30, -30])
    if k % 512:
        return np.exp2(np.random.permutation(np.resize(levels, k // 32))).repeat(32)
    a = np.empty((k // 512, 16))
    for p in range(k // 512):
        a[p, :8] = np.random.permutation(np.resize(levels, 8))
        for g in range(8):
            far = levels[np.abs(levels - a[p, g]) >= 10]
            a[p, g + 8] = far[np.random.randint(len(far))]
    return np.exp2(a.ravel()).repeat(32)


BF16 = ml_dtypes.bfloat16


def bf(x):
    return np.asarray(x, np.float32).astype(BF16)


def f64(x):
    return np.asarray(x).astype(np.float64)


B, S, DM, H, D, NQKV = 2, 512, 1024, 16, 64, 3
D2 = D // 2


def rope(t, c, s):
    t1, t2 = t[..., :D2], t[..., D2:]
    return np.concatenate([t1 * c - t2 * s, t1 * s + t2 * c], axis=-1)


def setup_inputs():
    s = mx_kscale(DM)
    ang = np.random.random((S, D2)) * 2.0 * np.pi
    return {"x": bf(np.random.standard_normal((B, S, DM)) * s),
            "qkv_w": bf(np.random.standard_normal((NQKV * H * D, DM)) / np.sqrt(DM) / s[None, :]),
            "rope_cos": bf(np.cos(ang)),
            "rope_sin": bf(np.sin(ang))}


def reference(x, qkv_w, rope_cos, rope_sin):
    qkv = (mxq(f64(x), 2, "e5m2") @ mxq(f64(qkv_w), 1, "e5m2").T).reshape(B, S, NQKV, H, D)
    q = qkv[:, :, 0].transpose(0, 2, 1, 3)
    k = qkv[:, :, 1].transpose(0, 2, 1, 3)
    v = qkv[:, :, 2].transpose(0, 2, 1, 3)
    c = f64(rope_cos)[None, None]
    s = f64(rope_sin)[None, None]
    return rope(q, c, s), rope(k, c, s), v

@@ -1,0 +1,270 @@
+from contextlib import ExitStack
+
+import concourse.mybir as mybir
+from concourse.masks import make_identity
+
+B, S, DM, H, D = 2, 512, 1024, 16, 64
+D2 = D // 2
+FLOPS = 2 * B * S * DM * 3 * H * D
+
+F32 = mybir.dt.float32
+BF16 = mybir.dt.bfloat16
+U32 = mybir.dt.uint32
+U8 = mybir.dt.uint8
+FP8X4 = mybir.dt.float8_e5m2_x4
+MUL = mybir.AluOpType.mult
+ADD = mybir.AluOpType.add
+
+P = 128
+NPASS = 2
+TPB = 4
+HG = 8
+NCOL = HG * D
+
+
+def tile_attention_pa_kernel(tc, x, qkv_w, rope_cos, rope_sin, out_0, out_1, out_2):
+    nc = tc.nc
+    outs = (out_0, out_1, out_2)
+
+    with ExitStack() as ctx:
+        const = ctx.enter_context(tc.tile_pool(name="const", bufs=1))
+        raw = ctx.enter_context(tc.tile_pool(name="raw", bufs=1))
+        codes = ctx.enter_context(tc.tile_pool(name="codes", bufs=1))
+        grp = ctx.enter_context(tc.tile_pool(name="grp", bufs=4))
+        stage = ctx.enter_context(tc.tile_pool(name="stage", bufs=3))
+        tps = ctx.enter_context(tc.psum_pool(name="tps", bufs=3))
+        accs = ctx.enter_context(tc.psum_pool(name="accs", bufs=5))
+
+        ident = const.tile([P, P], F32, name="ident")
+        make_identity(nc, ident[:])
+
+        ctx.enter_context(tc.manual_schedule())
+
+        cos_bf = const.tile([P, TPB, D2], BF16, name="cos_bf")
+        sin_bf = const.tile([P, TPB, D2], BF16, name="sin_bf")
+        nc.scalar.dma_start(out=cos_bf[:], in_=rope_cos.rearrange("(p t) j -> p t j", t=TPB))
+        nc.scalar.dma_start(out=sin_bf[:], in_=rope_sin.rearrange("(p t) j -> p t j", t=TPB))
+
+        def w_rows(n):
+            base = (n[0] * H + n[1] * HG) * D
+            return qkv_w[base : base + NCOL, :].rearrange("(p r) k -> p r k", r=4)
+
+        Q0, K0, V0, Q1, K1, V1 = (0, 0), (1, 0), (2, 0), (0, 1), (1, 1), (2, 1)
+        w_raw = {}
+        x_raw = {}
+
+        first = []
+        for rp in range(2):
+            half = raw.tile([P, 2, DM], BF16, name="w_first%d" % rp)
+            nc.sync.dma_start(out=half[:], in_=w_rows(Q0)[:, 2 * rp : 2 * rp + 2, :])
+            first.append(half)
+        w_raw[Q0] = first
+        for b in range(B):
+            rows = x[b].rearrange("(p t) k -> p t k", t=TPB)
+            for c in range(2):
+                if (b, c) == (0, 0):
+                    pair = []
+                    for i in range(2):
+                        one = raw.tile([P, DM], BF16, name="x_first%d" % i)
+                        nc.sync.dma_start(out=one[:], in_=rows[:, i, :])
+                        pair.append(one[:])
+                    x_raw[(b, c)] = pair
+                else:
+                    xt = raw.tile([P, 2, DM], BF16, name="x_raw%d%d" % (b, c))
+                    nc.sync.dma_start(out=xt[:], in_=rows[:, 2 * c : 2 * c + 2, :])
+                    x_raw[(b, c)] = [xt[:, 0, :], xt[:, 1, :]]
+        for n in (K0, V0, Q1, V1, K1):
+            wt = raw.tile([P, 4, DM], BF16, name="w_raw%d%d" % n)
+            nc.sync.dma_start(out=wt[:], in_=w_rows(n))
+            w_raw[n] = [wt[:, 0:2, :], wt[:, 2:4, :]]
+
+        warm = const.tile([P, 8], F32, name="warm")
+        warm2 = const.tile([P, 8], F32, name="warm2")
+        nc.vector.memset(warm[:], 0.0)
+        nc.scalar.copy(out=warm2[:], in_=warm[:])
+        cc = const.tile([P, TPB, D], F32, name="cc")
+        ss = const.tile([P, TPB, D], F32, name="ss")
+        nc.gpsimd.tensor_copy(out=cc[:, :, 0:D2], in_=cos_bf[:])
+        nc.gpsimd.tensor_copy(out=cc[:, :, D2:D], in_=cos_bf[:])
+        nc.gpsimd.tensor_scalar_mul(out=ss[:, :, 0:D2], in0=sin_bf[:], scalar1=-1.0)
+        nc.gpsimd.tensor_copy(out=ss[:, :, D2:D], in_=sin_bf[:])
+
+        wq = {}
+        ws = {}
+        for n in (Q0, K0, V0, Q1, K1, V1):
+            wq[n] = codes.tile([P, NPASS, NCOL], U32, name="wq%d%d" % n, align_bytes=64)
+            ws[n] = codes.tile([P, NPASS, NCOL], U8, name="ws%d%d" % n, align_bytes=64)
+        xq = {}
+        xs = {}
+        for b in range(B):
+            for c in range(2):
+                xq[(b, c)] = codes.tile([P, 2, NPASS, P], U32, name="xq%d%d" % (b, c), align_bytes=64)
+                xs[(b, c)] = codes.tile([P, 2, NPASS, P], U8, name="xs%d%d" % (b, c), align_bytes=64)
+
+        def copy_on(eng, out, in_):
+            if eng == "v":
+                nc.vector.tensor_copy(out=out, in_=in_)
+            else:
+                nc.scalar.copy(out=out, in_=in_)
+
+        def transpose_bank(parts):
+            bank = tps.tile([P, 4, P], F32, name="tp")
+            for i in range(2):
+                words = parts[i][0].bitcast(F32)
+                g = parts[i][1]
+                for u in range(2):
+                    nc.tensor.transpose(bank[:, 2 * i + u, :], words[:, 256 * g + u : 256 * (g + 1) : 2], ident[:])
+            return bank
+
+        def w_bank(n, rp, g):
+            return transpose_bank([(w_raw[n][rp][:, i, :], g) for i in range(2)])
+
+        def w_evac(bank, gw, rp, eng):
+            dst = gw[:].bitcast(F32).rearrange("p (m r u) -> p m r u", r=4, u=2)[:, :, 2 * rp : 2 * rp + 2, :]
+            copy_on(eng, dst, bank[:].rearrange("p (r u) m -> p m r u", u=2))
+
+        def w_quant(n, g, gw):
+            nc.vector.quantize_mx(out=wq[n][:, g, :].bitcast(FP8X4), scales=ws[n][:, g, :], in_=gw[:])
+
+        pending = []
+
+        def w_run(n, g, engs):
+            gw = grp.tile([P, 4 * NCOL], BF16, name="gw", align_bytes=64)
+            banks = [w_bank(n, rp, g) for rp in range(2)]
+            for rp in range(2):
+                w_evac(banks[rp], gw, rp, engs[rp])
+            pending.append(lambda: w_quant(n, g, gw))
+
+        def x_quant(bc, gx, i0, i1):
+            nc.vector.quantize_mx(
+                out=xq[bc][:, i0:i1].rearrange("p t g c -> p (t g c)").bitcast(FP8X4),
+                scales=xs[bc][:, i0:i1].rearrange("p t g c -> p (t g c)"),
+                in_=gx[:, i0 * 2 * NCOL : i1 * 2 * NCOL],
+            )
+
+        def x_tile(bc, i, gx, eng):
+            bank = transpose_bank([(x_raw[bc][i], g) for g in range(NPASS)])
+            view = gx[:].bitcast(F32).rearrange("p (t g m u) -> p t g m u", t=2, g=NPASS, u=2)
+            return lambda: copy_on(eng, view[:, i], bank[:].rearrange("p (g u) m -> p g m u", u=2))
+
+        def x_run(bc, engs):
+            gx = grp.tile([P, 4 * NCOL], BF16, name="gx", align_bytes=64)
+            evacs = [x_tile(bc, i, gx, engs[i]) for i in range(2)]
+            for call in evacs:
+                call()
+            pending.append(lambda: x_quant(bc, gx, 0, 2))
+
+        def mm(n, b, t):
+            acc = accs.tile([P, NCOL], F32, name="acc")
+            bc = (b, t // 2)
+            for g in range(NPASS):
+                nc.tensor.matmul_mx(
+                    out=acc[:],
+                    lhsT=xq[bc][:, t % 2, g, :].bitcast(FP8X4),
+                    lhsT_scale=xs[bc][:, t % 2, g, :],
+                    rhs=wq[n][:, g, :].bitcast(FP8X4),
+                    rhs_scale=ws[n][:, g, :],
+                    start=(g == 0),
+                    stop=(g == NPASS - 1),
+                )
+            return acc
+
+        def store(n, b, tile_, t0, t1):
+            h0 = n[1] * HG
+            dst = outs[n[0]][b, h0 : h0 + HG].rearrange("h (p t) d -> p h t d", t=TPB)[:, :, t0:t1, :]
+            nc.sync.dma_start(
+                out=dst.rearrange("p h t d -> p h (t d)"),
+                in_=tile_[:, :, t0:t1, :].rearrange("p h t d -> p h (t d)"),
+            )
+
+        def rope_mults(acc, t, ta, tb):
+            nc.vector.tensor_tensor(
+                out=ta[:, :, t, :],
+                in0=acc[:].rearrange("p (h d) -> p h d", d=D),
+                in1=cc[:, t, :].unsqueeze(1).to_broadcast([P, HG, D]),
+                op=MUL,
+            )
+            nc.vector.tensor_tensor(
+                out=tb[:, :, t, :].rearrange("p h (f j) -> p h f j", f=2),
+                in0=acc[:].rearrange("p (h f j) -> p h f j", f=2, j=D2)[:, :, ::-1, :],
+                in1=ss[:, t, :].rearrange("p (f j) -> p f j", f=2).unsqueeze(1).to_broadcast([P, HG, 2, D2]),
+                op=MUL,
+            )
+
+        gw_first = [grp.tile([P, 4 * NCOL], BF16, name="gw", align_bytes=64) for g in range(NPASS)]
+        for rp in range(2):
+            banks = [w_bank(Q0, rp, g) for g in range(NPASS)]
+            for g in range(NPASS):
+                w_evac(banks[g], gw_first[g], rp, "vs"[g])
+        w_quant(Q0, 1, gw_first[1])
+        w_quant(Q0, 0, gw_first[0])
+        gx_first = grp.tile([P, 4 * NCOL], BF16, name="gx", align_bytes=64)
+        for i in range(2):
+            x_tile((0, 0), i, gx_first, "s")()
+            x_quant((0, 0), gx_first, i, i + 1)
+        x_run((0, 1), "vs")
+
+        runs = {
+            0: [("x", (1, 0)), ("x", (1, 1))],
+            1: [("w", K0, 0), ("w", K0, 1)],
+            2: [("w", V0, 0), ("w", V0, 1)],
+            3: [("w", Q1, 0)],
+            4: [("w", Q1, 1)],
+            5: [("w", V1, 0)],
+            6: [("w", V1, 1)],
+            7: [("w", K1, 0)],
+            8: [("w", K1, 1)],
+        }
+        copies_in_slot = [0, 0, 0, 0, 1, 1, 1, 1, 1, 2, 2, 2, 2, 2, 1, 0]
+        copy_units = [(n, b, t) for n in (V0, V1) for b in range(B) for t in range(TPB)]
+        rope_groups = (Q0, K0, Q1, K1)
+        state = {"copy": 0}
+        vtile = {}
+        rtile = {}
+
+        for s in range(16):
+            n = rope_groups[s // 4]
+            b = (s // 2) % 2
+            t0 = 2 * (s % 2)
+            last = s == 15
+            if t0 == 0:
+                rtile["a"] = stage.tile([P, HG, TPB, D], F32, name="ra")
+                rtile["b"] = stage.tile([P, HG, TPB, D], F32, name="rb")
+            ta = rtile["a"]
+            tb = rtile["b"]
+
+            acc_r = [mm(n, b, t0), mm(n, b, t0 + 1)]
+            for i in range(copies_in_slot[s]):
+                cn, cb, ct = copy_units[state["copy"]]
+                state["copy"] += 1
+                if ct == 0:
+                    vtile["v"] = stage.tile([P, HG, TPB, D], F32, name="vv")
+                acc_c = mm(cn, cb, ct)
+                nc.scalar.copy(out=vtile["v"][:, :, ct, :], in_=acc_c[:].rearrange("p (h d) -> p h d", d=D))
+                if ct == TPB - 1:
+                    store(cn, cb, vtile["v"], 0, TPB)
+
+            flush_now = list(pending)
+            pending.clear()
+            for item in runs.get(s, []):
+                if item[0] == "x":
+                    x_run(item[1], "ss")
+                else:
+                    w_run(item[1], item[2], "ss")
+            for call in flush_now:
+                call()
+
+            for i in range(2):
+                rope_mults(acc_r[i], t0 + i, ta, tb)
+                if last:
+                    eng = (nc.gpsimd, nc.vector)[i]
+                    eng.tensor_tensor(out=ta[:, :, t0 + i, :], in0=ta[:, :, t0 + i, :], in1=tb[:, :, t0 + i, :], op=ADD)
+                    store(n, b, ta, t0 + i, t0 + i + 1)
+            if not last:
+                nc.gpsimd.tensor_tensor(
+                    out=ta[:, :, t0 : t0 + 2, :], in0=ta[:, :, t0 : t0 + 2, :], in1=tb[:, :, t0 : t0 + 2, :], op=ADD
+                )
+                if s == 14:
+                    store(n, b, ta, 0, 2)
+                elif t0 == 2:
+                    store(n, b, ta, 0, TPB)

@@ -81,6 +81,8 @@ def tile_attention_pa_kernel(tc, x, qkv_w, rope_cos, rope_sin, out_0, out_1, out
         warm = const.tile([P, 8], F32, name="warm")
         warm2 = const.tile([P, 8], F32, name="warm2")
         nc.vector.memset(warm[:], 0.0)
+        zeros = const.tile([P, NCOL], BF16, name="zeros")
+        nc.vector.memset(zeros[:], 0.0)
         nc.scalar.copy(out=warm2[:], in_=warm[:])
         cc = const.tile([P, TPB, D], F32, name="cc")
         ss = const.tile([P, TPB, D], F32, name="ss")
@@ -100,6 +102,10 @@ def tile_attention_pa_kernel(tc, x, qkv_w, rope_cos, rope_sin, out_0, out_1, out
             for c in range(2):
                 xq[(b, c)] = codes.tile([P, 2, NPASS, P], U32, name="xq%d%d" % (b, c), align_bytes=64)
                 xs[(b, c)] = codes.tile([P, 2, NPASS, P], U8, name="xs%d%d" % (b, c), align_bytes=64)
+
+        def warm_up():
+            junk = accs.tile([P, NCOL], F32, name="acc")
+            nc.tensor.matmul(out=junk[:], lhsT=zeros[:, 0:P], rhs=zeros[:], start=True, stop=True)
 
         def copy_on(eng, out, in_):
             if eng == "v":
@@ -150,6 +156,7 @@ def tile_attention_pa_kernel(tc, x, qkv_w, rope_cos, rope_sin, out_0, out_1, out
         def x_run(bc, engs):
             gx = grp.tile([P, 4 * NCOL], BF16, name="gx", align_bytes=64)
             evacs = [x_tile(bc, i, gx, engs[i]) for i in range(2)]
+            warm_up()
             for call in evacs:
                 call()
             pending.append(lambda: x_quant(bc, gx, 0, 2))
@@ -191,80 +198,73 @@ def tile_attention_pa_kernel(tc, x, qkv_w, rope_cos, rope_sin, out_0, out_1, out
                 op=MUL,
             )
 
+        for i in range(6):
+            warm_up()
+
         gw_first = [grp.tile([P, 4 * NCOL], BF16, name="gw", align_bytes=64) for g in range(NPASS)]
         for rp in range(2):
             banks = [w_bank(Q0, rp, g) for g in range(NPASS)]
+            warm_up()
             for g in range(NPASS):
                 w_evac(banks[g], gw_first[g], rp, "vs"[g])
         w_quant(Q0, 1, gw_first[1])
         w_quant(Q0, 0, gw_first[0])
         gx_first = grp.tile([P, 4 * NCOL], BF16, name="gx", align_bytes=64)
         for i in range(2):
-            x_tile((0, 0), i, gx_first, "s")()
+            evac = x_tile((0, 0), i, gx_first, "s")
+            warm_up()
+            evac()
             x_quant((0, 0), gx_first, i, i + 1)
         x_run((0, 1), "vs")
+        x_run((1, 0), "ss")
+        x_run((1, 1), "ss")
+        for call in pending[0:2]:
+            call()
+        late = pending[2:]
+        pending.clear()
+        pending.extend(late)
 
-        runs = {
-            0: [("x", (1, 0)), ("x", (1, 1))],
-            1: [("w", K0, 0), ("w", K0, 1)],
-            2: [("w", V0, 0), ("w", V0, 1)],
-            3: [("w", Q1, 0)],
-            4: [("w", Q1, 1)],
-            5: [("w", V1, 0)],
-            6: [("w", V1, 1)],
-            7: [("w", K1, 0)],
-            8: [("w", K1, 1)],
-        }
-        copies_in_slot = [0, 0, 0, 0, 1, 1, 1, 1, 1, 2, 2, 2, 2, 2, 1, 0]
+        later_runs = [(n, g) for n in (K0, V0, Q1, V1, K1) for g in range(NPASS)]
         copy_units = [(n, b, t) for n in (V0, V1) for b in range(B) for t in range(TPB)]
-        rope_groups = (Q0, K0, Q1, K1)
-        state = {"copy": 0}
-        vtile = {}
-        rtile = {}
+        rope_units = [(n, b, t) for n in (Q0, K0, Q1, K1) for b in range(B) for t in range(TPB)]
+        FIRST_COPY = 10
+        acc_of = {}
+        held = {}
 
-        for s in range(16):
-            n = rope_groups[s // 4]
-            b = (s // 2) % 2
-            t0 = 2 * (s % 2)
-            last = s == 15
-            if t0 == 0:
-                rtile["a"] = stage.tile([P, HG, TPB, D], F32, name="ra")
-                rtile["b"] = stage.tile([P, HG, TPB, D], F32, name="rb")
-            ta = rtile["a"]
-            tb = rtile["b"]
+        for u in range(2):
+            acc_of[u] = mm(*rope_units[u])
 
-            acc_r = [mm(n, b, t0), mm(n, b, t0 + 1)]
-            for i in range(copies_in_slot[s]):
-                cn, cb, ct = copy_units[state["copy"]]
-                state["copy"] += 1
+        for u in range(len(rope_units)):
+            n, b, t = rope_units[u]
+            if u % 2 == 0:
+                if u > 0:
+                    for call in pending:
+                        call()
+                    pending.clear()
+                if u // 2 < len(later_runs):
+                    w_run(later_runs[u // 2][0], later_runs[u // 2][1], "ss")
+            if FIRST_COPY <= u < FIRST_COPY + len(copy_units):
+                cn, cb, ct = copy_units[u - FIRST_COPY]
                 if ct == 0:
-                    vtile["v"] = stage.tile([P, HG, TPB, D], F32, name="vv")
+                    held["v"] = stage.tile([P, HG, TPB, D], F32, name="vv")
                 acc_c = mm(cn, cb, ct)
-                nc.scalar.copy(out=vtile["v"][:, :, ct, :], in_=acc_c[:].rearrange("p (h d) -> p h d", d=D))
+                nc.scalar.copy(out=held["v"][:, :, ct, :], in_=acc_c[:].rearrange("p (h d) -> p h d", d=D))
                 if ct == TPB - 1:
-                    store(cn, cb, vtile["v"], 0, TPB)
-
-            flush_now = list(pending)
-            pending.clear()
-            for item in runs.get(s, []):
-                if item[0] == "x":
-                    x_run(item[1], "ss")
-                else:
-                    w_run(item[1], item[2], "ss")
-            for call in flush_now:
-                call()
-
-            for i in range(2):
-                rope_mults(acc_r[i], t0 + i, ta, tb)
-                if last:
-                    eng = (nc.gpsimd, nc.vector)[i]
-                    eng.tensor_tensor(out=ta[:, :, t0 + i, :], in0=ta[:, :, t0 + i, :], in1=tb[:, :, t0 + i, :], op=ADD)
-                    store(n, b, ta, t0 + i, t0 + i + 1)
-            if not last:
+                    store(cn, cb, held["v"], 0, TPB)
+            if u + 2 < len(rope_units):
+                acc_of[u + 2] = mm(*rope_units[u + 2])
+            if t == 0:
+                held["a"] = stage.tile([P, HG, TPB, D], F32, name="ra")
+                held["b"] = stage.tile([P, HG, TPB, D], F32, name="rb")
+            ta = held["a"]
+            tb = held["b"]
+            rope_mults(acc_of[u], t, ta, tb)
+            if u >= len(rope_units) - 2:
+                eng = nc.gpsimd if u % 2 == 0 else nc.vector
+                eng.tensor_tensor(out=ta[:, :, t, :], in0=ta[:, :, t, :], in1=tb[:, :, t, :], op=ADD)
+            elif u % 2 == 1:
                 nc.gpsimd.tensor_tensor(
-                    out=ta[:, :, t0 : t0 + 2, :], in0=ta[:, :, t0 : t0 + 2, :], in1=tb[:, :, t0 : t0 + 2, :], op=ADD
+                    out=ta[:, :, t - 1 : t + 1, :], in0=ta[:, :, t - 1 : t + 1, :], in1=tb[:, :, t - 1 : t + 1, :], op=ADD
                 )
-                if s == 14:
-                    store(n, b, ta, 0, 2)
-                elif t0 == 2:
-                    store(n, b, ta, 0, TPB)
+            if t == TPB - 1:
+                store(n, b, ta, 0, TPB)

@@ -156,7 +156,6 @@ def tile_attention_pa_kernel(tc, x, qkv_w, rope_cos, rope_sin, out_0, out_1, out
         def x_run(bc, engs):
             gx = grp.tile([P, 4 * NCOL], BF16, name="gx", align_bytes=64)
             evacs = [x_tile(bc, i, gx, engs[i]) for i in range(2)]
-            warm_up()
             for call in evacs:
                 call()
             pending.append(lambda: x_quant(bc, gx, 0, 2))
@@ -204,7 +203,6 @@ def tile_attention_pa_kernel(tc, x, qkv_w, rope_cos, rope_sin, out_0, out_1, out
         gw_first = [grp.tile([P, 4 * NCOL], BF16, name="gw", align_bytes=64) for g in range(NPASS)]
         for rp in range(2):
             banks = [w_bank(Q0, rp, g) for g in range(NPASS)]
-            warm_up()
             for g in range(NPASS):
                 w_evac(banks[g], gw_first[g], rp, "vs"[g])
         w_quant(Q0, 1, gw_first[1])
@@ -212,7 +210,6 @@ def tile_attention_pa_kernel(tc, x, qkv_w, rope_cos, rope_sin, out_0, out_1, out
         gx_first = grp.tile([P, 4 * NCOL], BF16, name="gx", align_bytes=64)
         for i in range(2):
             evac = x_tile((0, 0), i, gx_first, "s")
-            warm_up()
             evac()
             x_quant((0, 0), gx_first, i, i + 1)
         x_run((0, 1), "vs")

@@ -219,7 +219,6 @@ def tile_attention_pa_kernel(tc, x, qkv_w, rope_cos, rope_sin, out_0, out_1, out
             call()
         late = pending[2:]
         pending.clear()
-        pending.extend(late)
 
         later_runs = [(n, g) for n in (K0, V0, Q1, V1, K1) for g in range(NPASS)]
         copy_units = [(n, b, t) for n in (V0, V1) for b in range(B) for t in range(TPB)]
@@ -240,6 +239,9 @@ def tile_attention_pa_kernel(tc, x, qkv_w, rope_cos, rope_sin, out_0, out_1, out
                     pending.clear()
                 if u // 2 < len(later_runs):
                     w_run(later_runs[u // 2][0], later_runs[u // 2][1], "ss")
+            if u == 1:
+                for call in late:
+                    call()
             if FIRST_COPY <= u < FIRST_COPY + len(copy_units):
                 cn, cb, ct = copy_units[u - FIRST_COPY]
                 if ct == 0:

@@ -91,11 +91,12 @@ def tile_attention_pa_kernel(tc, x, qkv_w, rope_cos, rope_sin, out_0, out_1, out
         nc.gpsimd.tensor_scalar_mul(out=ss[:, :, 0:D2], in0=sin_bf[:], scalar1=-1.0)
         nc.gpsimd.tensor_copy(out=ss[:, :, D2:D], in_=sin_bf[:])
 
-        wq = {}
-        ws = {}
-        for n in (Q0, K0, V0, Q1, K1, V1):
-            wq[n] = codes.tile([P, NPASS, NCOL], U32, name="wq%d%d" % n, align_bytes=64)
-            ws[n] = codes.tile([P, NPASS, NCOL], U8, name="ws%d%d" % n, align_bytes=64)
+        made = [Q0, K0, V0, Q1, V1, K1]
+        wq = codes.tile([P, NPASS * len(made), NCOL], U32, name="wq", align_bytes=64)
+        ws = codes.tile([P, NPASS * len(made), NCOL], U8, name="ws", align_bytes=64)
+
+        def slot(n, g):
+            return NPASS * made.index(n) + g
         xq = {}
         xs = {}
         for b in range(B):
@@ -126,20 +127,22 @@ def tile_attention_pa_kernel(tc, x, qkv_w, rope_cos, rope_sin, out_0, out_1, out
             return transpose_bank([(w_raw[n][rp][:, i, :], g) for i in range(2)])
 
         def w_evac(bank, gw, rp, eng):
-            dst = gw[:].bitcast(F32).rearrange("p (m r u) -> p m r u", r=4, u=2)[:, :, 2 * rp : 2 * rp + 2, :]
+            dst = gw.bitcast(F32).rearrange("p (m r u) -> p m r u", r=4, u=2)[:, :, 2 * rp : 2 * rp + 2, :]
             copy_on(eng, dst, bank[:].rearrange("p (r u) m -> p m r u", u=2))
 
-        def w_quant(n, g, gw):
-            nc.vector.quantize_mx(out=wq[n][:, g, :].bitcast(FP8X4), scales=ws[n][:, g, :], in_=gw[:])
+        def w_quant(first, count, gw):
+            nc.vector.quantize_mx(
+                out=wq[:, first : first + count, :].rearrange("p s c -> p (s c)").bitcast(FP8X4),
+                scales=ws[:, first : first + count, :].rearrange("p s c -> p (s c)"),
+                in_=gw[:].rearrange("p s c -> p (s c)"),
+            )
 
         pending = []
 
-        def w_run(n, g, engs):
-            gw = grp.tile([P, 4 * NCOL], BF16, name="gw", align_bytes=64)
+        def w_run(n, g, part):
             banks = [w_bank(n, rp, g) for rp in range(2)]
             for rp in range(2):
-                w_evac(banks[rp], gw, rp, engs[rp])
-            pending.append(lambda: w_quant(n, g, gw))
+                w_evac(banks[rp], part, rp, "s")
 
         def x_quant(bc, gx, i0, i1):
             nc.vector.quantize_mx(
@@ -168,20 +171,17 @@ def tile_attention_pa_kernel(tc, x, qkv_w, rope_cos, rope_sin, out_0, out_1, out
                     out=acc[:],
                     lhsT=xq[bc][:, t % 2, g, :].bitcast(FP8X4),
                     lhsT_scale=xs[bc][:, t % 2, g, :],
-                    rhs=wq[n][:, g, :].bitcast(FP8X4),
-                    rhs_scale=ws[n][:, g, :],
+                    rhs=wq[:, slot(n, g), :].bitcast(FP8X4),
+                    rhs_scale=ws[:, slot(n, g), :],
                     start=(g == 0),
                     stop=(g == NPASS - 1),
                 )
             return acc
 
-        def store(n, b, tile_, t0, t1):
+        def store(queue, n, b, tile_, ha, hb):
             h0 = n[1] * HG
-            dst = outs[n[0]][b, h0 : h0 + HG].rearrange("h (p t) d -> p h t d", t=TPB)[:, :, t0:t1, :]
-            nc.sync.dma_start(
-                out=dst.rearrange("p h t d -> p h (t d)"),
-                in_=tile_[:, :, t0:t1, :].rearrange("p h t d -> p h (t d)"),
-            )
+            dst = outs[n[0]][b, h0 + ha : h0 + hb].rearrange("h (p t) d -> p h t d", t=TPB)
+            queue.dma_start(out=dst.rearrange("p h t d -> p h (t d)"), in_=tile_[:, ha:hb].rearrange("p h t d -> p h (t d)"))
 
         def rope_mults(acc, t, ta, tb):
             nc.vector.tensor_tensor(
@@ -200,13 +200,13 @@ def tile_attention_pa_kernel(tc, x, qkv_w, rope_cos, rope_sin, out_0, out_1, out
         for i in range(6):
             warm_up()
 
-        gw_first = [grp.tile([P, 4 * NCOL], BF16, name="gw", align_bytes=64) for g in range(NPASS)]
+        gw_first = [grp.tile([P, 1, 4 * NCOL], BF16, name="gw", align_bytes=64) for g in range(NPASS)]
         for rp in range(2):
             banks = [w_bank(Q0, rp, g) for g in range(NPASS)]
             for g in range(NPASS):
-                w_evac(banks[g], gw_first[g], rp, "vs"[g])
-        w_quant(Q0, 1, gw_first[1])
-        w_quant(Q0, 0, gw_first[0])
+                w_evac(banks[g], gw_first[g][:, 0, :], rp, "vs"[g])
+        w_quant(slot(Q0, 1), 1, gw_first[1])
+        w_quant(slot(Q0, 0), 1, gw_first[0])
         gx_first = grp.tile([P, 4 * NCOL], BF16, name="gx", align_bytes=64)
         for i in range(2):
             evac = x_tile((0, 0), i, gx_first, "s")
@@ -220,11 +220,14 @@ def tile_attention_pa_kernel(tc, x, qkv_w, rope_cos, rope_sin, out_0, out_1, out
         late = pending[2:]
         pending.clear()
 
-        later_runs = [(n, g) for n in (K0, V0, Q1, V1, K1) for g in range(NPASS)]
+        later_runs = [(n, g) for n in made[1:] for g in range(NPASS)]
+        run_step = [2 * j for j in range(len(later_runs))]
+        quant_step = [TPB * ((s + TPB + 1) // TPB) for s in run_step]
         copy_units = [(n, b, t) for n in (V0, V1) for b in range(B) for t in range(TPB)]
         rope_units = [(n, b, t) for n in (Q0, K0, Q1, K1) for b in range(B) for t in range(TPB)]
         FIRST_COPY = 10
         acc_of = {}
+        gw_of = {}
         held = {}
 
         for u in range(2):
@@ -232,16 +235,20 @@ def tile_attention_pa_kernel(tc, x, qkv_w, rope_cos, rope_sin, out_0, out_1, out
 
         for u in range(len(rope_units)):
             n, b, t = rope_units[u]
-            if u % 2 == 0:
-                if u > 0:
-                    for call in pending:
-                        call()
-                    pending.clear()
-                if u // 2 < len(later_runs):
-                    w_run(later_runs[u // 2][0], later_runs[u // 2][1], "ss")
             if u == 1:
                 for call in late:
                     call()
+            sharing = [j for j in range(len(later_runs)) if quant_step[j] == u]
+            if sharing:
+                w_quant(slot(*later_runs[sharing[0]]), len(sharing), gw_of[sharing[0]])
+            if u in run_step:
+                j = run_step.index(u)
+                sharing = [i for i in range(len(later_runs)) if quant_step[i] == quant_step[j]]
+                if j == sharing[0]:
+                    shared = grp.tile([P, len(sharing), 4 * NCOL], BF16, name="gw", align_bytes=64)
+                    for i in sharing:
+                        gw_of[i] = shared
+                w_run(later_runs[j][0], later_runs[j][1], gw_of[j][:, j - sharing[0], :])
             if FIRST_COPY <= u < FIRST_COPY + len(copy_units):
                 cn, cb, ct = copy_units[u - FIRST_COPY]
                 if ct == 0:
@@ -249,21 +256,30 @@ def tile_attention_pa_kernel(tc, x, qkv_w, rope_cos, rope_sin, out_0, out_1, out
                 acc_c = mm(cn, cb, ct)
                 nc.scalar.copy(out=held["v"][:, :, ct, :], in_=acc_c[:].rearrange("p (h d) -> p h d", d=D))
                 if ct == TPB - 1:
-                    store(cn, cb, held["v"], 0, TPB)
+                    store(nc.scalar, cn, cb, held["v"], 0, HG)
             if u + 2 < len(rope_units):
                 acc_of[u + 2] = mm(*rope_units[u + 2])
             if t == 0:
-                held["a"] = stage.tile([P, HG, TPB, D], F32, name="ra")
+                held["a"] = stage.tile([P, HG, TPB, D], F32, name="ra", bufs=4)
                 held["b"] = stage.tile([P, HG, TPB, D], F32, name="rb")
             ta = held["a"]
             tb = held["b"]
             rope_mults(acc_of[u], t, ta, tb)
-            if u >= len(rope_units) - 2:
-                eng = nc.gpsimd if u % 2 == 0 else nc.vector
-                eng.tensor_tensor(out=ta[:, :, t, :], in0=ta[:, :, t, :], in1=tb[:, :, t, :], op=ADD)
-            elif u % 2 == 1:
+            if t == TPB - 1 and u < len(rope_units) - 1:
                 nc.gpsimd.tensor_tensor(
-                    out=ta[:, :, t - 1 : t + 1, :], in0=ta[:, :, t - 1 : t + 1, :], in1=tb[:, :, t - 1 : t + 1, :], op=ADD
+                    out=ta[:].rearrange("p h t d -> p (h t d)"),
+                    in0=ta[:].rearrange("p h t d -> p (h t d)"),
+                    in1=tb[:].rearrange("p h t d -> p (h t d)"),
+                    op=ADD,
                 )
-            if t == TPB - 1:
-                store(n, b, ta, 0, TPB)
+                store(nc.sync, n, b, ta, 0, HG)
+            elif t == TPB - 1:
+                for ha in (0, HG // 2):
+                    hb = ha + HG // 2
+                    nc.vector.tensor_tensor(
+                        out=ta[:, ha:hb].rearrange("p h t d -> p (h t d)"),
+                        in0=ta[:, ha:hb].rearrange("p h t d -> p (h t d)"),
+                        in1=tb[:, ha:hb].rearrange("p h t d -> p (h t d)"),
+                        op=ADD,
+                    )
+                    store(nc.sync, n, b, ta, ha, hb)

@@ -265,18 +265,14 @@ def tile_attention_pa_kernel(tc, x, qkv_w, rope_cos, rope_sin, out_0, out_1, out
             ta = held["a"]
             tb = held["b"]
             rope_mults(acc_of[u], t, ta, tb)
-            if t == TPB - 1 and u < len(rope_units) - 1:
-                nc.gpsimd.tensor_tensor(
-                    out=ta[:].rearrange("p h t d -> p (h t d)"),
-                    in0=ta[:].rearrange("p h t d -> p (h t d)"),
-                    in1=tb[:].rearrange("p h t d -> p (h t d)"),
-                    op=ADD,
-                )
-                store(nc.sync, n, b, ta, 0, HG)
-            elif t == TPB - 1:
-                for ha in (0, HG // 2):
-                    hb = ha + HG // 2
-                    nc.vector.tensor_tensor(
+            if t == TPB - 1:
+                last = len(rope_units) - 1
+                adder = nc.vector if u == last else nc.gpsimd
+                pieces = 2 if u >= last - TPB else 1
+                for piece in range(pieces):
+                    ha = piece * HG // pieces
+                    hb = ha + HG // pieces
+                    adder.tensor_tensor(
                         out=ta[:, ha:hb].rearrange("p h t d -> p (h t d)"),
                         in0=ta[:, ha:hb].rearrange("p h t d -> p (h t d)"),
                         in1=tb[:, ha:hb].rearrange("p h t d -> p (h t d)"),

@@ -84,12 +84,11 @@ def tile_attention_pa_kernel(tc, x, qkv_w, rope_cos, rope_sin, out_0, out_1, out
         zeros = const.tile([P, NCOL], BF16, name="zeros")
         nc.vector.memset(zeros[:], 0.0)
         nc.scalar.copy(out=warm2[:], in_=warm[:])
-        cc = const.tile([P, TPB, D], F32, name="cc")
-        ss = const.tile([P, TPB, D], F32, name="ss")
-        nc.gpsimd.tensor_copy(out=cc[:, :, 0:D2], in_=cos_bf[:])
-        nc.gpsimd.tensor_copy(out=cc[:, :, D2:D], in_=cos_bf[:])
-        nc.gpsimd.tensor_scalar_mul(out=ss[:, :, 0:D2], in0=sin_bf[:], scalar1=-1.0)
-        nc.gpsimd.tensor_copy(out=ss[:, :, D2:D], in_=sin_bf[:])
+        tab = const.tile([P, TPB, 2, D], F32, name="tab")
+        nc.gpsimd.tensor_copy(out=tab[:, :, 0, 0:D2], in_=cos_bf[:])
+        nc.gpsimd.tensor_copy(out=tab[:, :, 0, D2:D], in_=cos_bf[:])
+        nc.gpsimd.tensor_copy(out=tab[:, :, 1, 0:D2], in_=sin_bf[:])
+        nc.gpsimd.tensor_scalar_mul(out=tab[:, :, 1, D2:D], in0=sin_bf[:], scalar1=-1.0)
 
         made = [Q0, K0, V0, Q1, V1, K1]
         wq = codes.tile([P, NPASS * len(made), NCOL], U32, name="wq", align_bytes=64)
@@ -183,17 +182,11 @@ def tile_attention_pa_kernel(tc, x, qkv_w, rope_cos, rope_sin, out_0, out_1, out
             dst = outs[n[0]][b, h0 + ha : h0 + hb].rearrange("h (p t) d -> p h t d", t=TPB)
             queue.dma_start(out=dst.rearrange("p h t d -> p h (t d)"), in_=tile_[:, ha:hb].rearrange("p h t d -> p h (t d)"))
 
-        def rope_mults(acc, t, ta, tb):
+        def rope_mults(acc, t, ab):
             nc.vector.tensor_tensor(
-                out=ta[:, :, t, :],
-                in0=acc[:].rearrange("p (h d) -> p h d", d=D),
-                in1=cc[:, t, :].unsqueeze(1).to_broadcast([P, HG, D]),
-                op=MUL,
-            )
-            nc.vector.tensor_tensor(
-                out=tb[:, :, t, :].rearrange("p h (f j) -> p h f j", f=2),
-                in0=acc[:].rearrange("p (h f j) -> p h f j", f=2, j=D2)[:, :, ::-1, :],
-                in1=ss[:, t, :].rearrange("p (f j) -> p f j", f=2).unsqueeze(1).to_broadcast([P, HG, 2, D2]),
+                out=ab[:, :, :, t, :].rearrange("p s h d -> p h s d"),
+                in0=acc[:].rearrange("p (h d) -> p h d", d=D).unsqueeze(2).to_broadcast([P, HG, 2, D]),
+                in1=tab[:, t].unsqueeze(1).to_broadcast([P, HG, 2, D]),
                 op=MUL,
             )
 
@@ -252,7 +245,7 @@ def tile_attention_pa_kernel(tc, x, qkv_w, rope_cos, rope_sin, out_0, out_1, out
             if FIRST_COPY <= u < FIRST_COPY + len(copy_units):
                 cn, cb, ct = copy_units[u - FIRST_COPY]
                 if ct == 0:
-                    held["v"] = stage.tile([P, HG, TPB, D], F32, name="vv")
+                    held["v"] = stage.tile([P, HG, TPB, D], F32, name="vv", bufs=2)
                 acc_c = mm(cn, cb, ct)
                 nc.scalar.copy(out=held["v"][:, :, ct, :], in_=acc_c[:].rearrange("p (h d) -> p h d", d=D))
                 if ct == TPB - 1:
@@ -260,11 +253,9 @@ def tile_attention_pa_kernel(tc, x, qkv_w, rope_cos, rope_sin, out_0, out_1, out
             if u + 2 < len(rope_units):
                 acc_of[u + 2] = mm(*rope_units[u + 2])
             if t == 0:
-                held["a"] = stage.tile([P, HG, TPB, D], F32, name="ra", bufs=4)
-                held["b"] = stage.tile([P, HG, TPB, D], F32, name="rb")
-            ta = held["a"]
-            tb = held["b"]
-            rope_mults(acc_of[u], t, ta, tb)
+                held["ab"] = stage.tile([P, 2, HG, TPB, D], F32, name="ab", bufs=4)
+            ab = held["ab"]
+            rope_mults(acc_of[u], t, ab)
             if t == TPB - 1:
                 last = len(rope_units) - 1
                 adder = nc.vector if u == last else nc.gpsimd
@@ -272,10 +263,7 @@ def tile_attention_pa_kernel(tc, x, qkv_w, rope_cos, rope_sin, out_0, out_1, out
                 for piece in range(pieces):
                     ha = piece * HG // pieces
                     hb = ha + HG // pieces
-                    adder.tensor_tensor(
-                        out=ta[:, ha:hb].rearrange("p h t d -> p (h t d)"),
-                        in0=ta[:, ha:hb].rearrange("p h t d -> p (h t d)"),
-                        in1=tb[:, ha:hb].rearrange("p h t d -> p (h t d)"),
-                        op=ADD,
-                    )
-                    store(nc.sync, n, b, ta, ha, hb)
+                    firsts = ab[:, 0, ha:hb].rearrange("p h t (f j) -> p (h t) f j", f=2)
+                    seconds = ab[:, 1, ha:hb].rearrange("p h t (f j) -> p (h t) f j", f=2)
+                    adder.tensor_tensor(out=firsts, in0=firsts, in1=seconds[:, :, ::-1, :], op=ADD)
+                    store(nc.sync, n, b, ab[:, 0], ha, hb)

@@ -223,6 +223,9 @@ def tile_attention_pa_kernel(tc, x, qkv_w, rope_cos, rope_sin, out_0, out_1, out
         gw_of = {}
         held = {}
 
+        for rp in range(2):
+            nc.sync.dma_start(out=first[rp][:], in_=w_rows(Q0)[:, 2 * rp : 2 * rp + 2, :])
+
         for u in range(2):
             acc_of[u] = mm(*rope_units[u])
 

from contextlib import ExitStack

import concourse.mybir as mybir
from concourse.masks import make_identity

B, S, DM, H, D = 2, 512, 1024, 16, 64
D2 = D // 2
FLOPS = 2 * B * S * DM * 3 * H * D

F32 = mybir.dt.float32
BF16 = mybir.dt.bfloat16
U32 = mybir.dt.uint32
U8 = mybir.dt.uint8
FP8X4 = mybir.dt.float8_e5m2_x4
MUL = mybir.AluOpType.mult
ADD = mybir.AluOpType.add

P = 128
NPASS = 2
TPB = 4
HG = 8
NCOL = HG * D


def tile_attention_pa_kernel(tc, x, qkv_w, rope_cos, rope_sin, out_0, out_1, out_2):
    nc = tc.nc
    outs = (out_0, out_1, out_2)

    with ExitStack() as ctx:
        const = ctx.enter_context(tc.tile_pool(name="const", bufs=1))
        raw = ctx.enter_context(tc.tile_pool(name="raw", bufs=1))
        codes = ctx.enter_context(tc.tile_pool(name="codes", bufs=1))
        grp = ctx.enter_context(tc.tile_pool(name="grp", bufs=4))
        stage = ctx.enter_context(tc.tile_pool(name="stage", bufs=3))
        tps = ctx.enter_context(tc.psum_pool(name="tps", bufs=3))
        accs = ctx.enter_context(tc.psum_pool(name="accs", bufs=5))

        ident = const.tile([P, P], F32, name="ident")
        make_identity(nc, ident[:])

        ctx.enter_context(tc.manual_schedule())

        cos_bf = const.tile([P, TPB, D2], BF16, name="cos_bf")
        sin_bf = const.tile([P, TPB, D2], BF16, name="sin_bf")
        nc.scalar.dma_start(out=cos_bf[:], in_=rope_cos.rearrange("(p t) j -> p t j", t=TPB))
        nc.scalar.dma_start(out=sin_bf[:], in_=rope_sin.rearrange("(p t) j -> p t j", t=TPB))

        def w_rows(n):
            base = (n[0] * H + n[1] * HG) * D
            return qkv_w[base : base + NCOL, :].rearrange("(p r) k -> p r k", r=4)

        Q0, K0, V0, Q1, K1, V1 = (0, 0), (1, 0), (2, 0), (0, 1), (1, 1), (2, 1)
        w_raw = {}
        x_raw = {}

        first = []
        for rp in range(2):
            half = raw.tile([P, 2, DM], BF16, name="w_first%d" % rp)
            nc.sync.dma_start(out=half[:], in_=w_rows(Q0)[:, 2 * rp : 2 * rp + 2, :])
            first.append(half)
        w_raw[Q0] = first
        for b in range(B):
            rows = x[b].rearrange("(p t) k -> p t k", t=TPB)
            for c in range(2):
                if (b, c) == (0, 0):
                    pair = []
                    for i in range(2):
                        one = raw.tile([P, DM], BF16, name="x_first%d" % i)
                        nc.sync.dma_start(out=one[:], in_=rows[:, i, :])
                        pair.append(one[:])
                    x_raw[(b, c)] = pair
                else:
                    xt = raw.tile([P, 2, DM], BF16, name="x_raw%d%d" % (b, c))
                    nc.sync.dma_start(out=xt[:], in_=rows[:, 2 * c : 2 * c + 2, :])
                    x_raw[(b, c)] = [xt[:, 0, :], xt[:, 1, :]]
        for n in (K0, V0, Q1, V1, K1):
            wt = raw.tile([P, 4, DM], BF16, name="w_raw%d%d" % n)
            nc.sync.dma_start(out=wt[:], in_=w_rows(n))
            w_raw[n] = [wt[:, 0:2, :], wt[:, 2:4, :]]

        warm = const.tile([P, 8], F32, name="warm")
        warm2 = const.tile([P, 8], F32, name="warm2")
        nc.vector.memset(warm[:], 0.0)
        zeros = const.tile([P, NCOL], BF16, name="zeros")
        nc.vector.memset(zeros[:], 0.0)
        nc.scalar.copy(out=warm2[:], in_=warm[:])
        tab = const.tile([P, TPB, 2, D], F32, name="tab")
        nc.gpsimd.tensor_copy(out=tab[:, :, 0, 0:D2], in_=cos_bf[:])
        nc.gpsimd.tensor_copy(out=tab[:, :, 0, D2:D], in_=cos_bf[:])
        nc.gpsimd.tensor_copy(out=tab[:, :, 1, 0:D2], in_=sin_bf[:])
        nc.gpsimd.tensor_scalar_mul(out=tab[:, :, 1, D2:D], in0=sin_bf[:], scalar1=-1.0)

        made = [Q0, K0, V0, Q1, V1, K1]
        wq = codes.tile([P, NPASS * len(made), NCOL], U32, name="wq", align_bytes=64)
        ws = codes.tile([P, NPASS * len(made), NCOL], U8, name="ws", align_bytes=64)

        def slot(n, g):
            return NPASS * made.index(n) + g
        xq = {}
        xs = {}
        for b in range(B):
            for c in range(2):
                xq[(b, c)] = codes.tile([P, 2, NPASS, P], U32, name="xq%d%d" % (b, c), align_bytes=64)
                xs[(b, c)] = codes.tile([P, 2, NPASS, P], U8, name="xs%d%d" % (b, c), align_bytes=64)

        def warm_up():
            junk = accs.tile([P, NCOL], F32, name="acc")
            nc.tensor.matmul(out=junk[:], lhsT=zeros[:, 0:P], rhs=zeros[:], start=True, stop=True)

        def copy_on(eng, out, in_):
            if eng == "v":
                nc.vector.tensor_copy(out=out, in_=in_)
            else:
                nc.scalar.copy(out=out, in_=in_)

        def transpose_bank(parts):
            bank = tps.tile([P, 4, P], F32, name="tp")
            for i in range(2):
                words = parts[i][0].bitcast(F32)
                g = parts[i][1]
                for u in range(2):
                    nc.tensor.transpose(bank[:, 2 * i + u, :], words[:, 256 * g + u : 256 * (g + 1) : 2], ident[:])
            return bank

        def w_bank(n, rp, g):
            return transpose_bank([(w_raw[n][rp][:, i, :], g) for i in range(2)])

        def w_evac(bank, gw, rp, eng):
            dst = gw.bitcast(F32).rearrange("p (m r u) -> p m r u", r=4, u=2)[:, :, 2 * rp : 2 * rp + 2, :]
            copy_on(eng, dst, bank[:].rearrange("p (r u) m -> p m r u", u=2))

        def w_quant(first, count, gw):
            nc.vector.quantize_mx(
                out=wq[:, first : first + count, :].rearrange("p s c -> p (s c)").bitcast(FP8X4),
                scales=ws[:, first : first + count, :].rearrange("p s c -> p (s c)"),
                in_=gw[:].rearrange("p s c -> p (s c)"),
            )

        pending = []

        def w_run(n, g, part):
            banks = [w_bank(n, rp, g) for rp in range(2)]
            for rp in range(2):
                w_evac(banks[rp], part, rp, "s")

        def x_quant(bc, gx, i0, i1):
            nc.vector.quantize_mx(
                out=xq[bc][:, i0:i1].rearrange("p t g c -> p (t g c)").bitcast(FP8X4),
                scales=xs[bc][:, i0:i1].rearrange("p t g c -> p (t g c)"),
                in_=gx[:, i0 * 2 * NCOL : i1 * 2 * NCOL],
            )

        def x_tile(bc, i, gx, eng):
            bank = transpose_bank([(x_raw[bc][i], g) for g in range(NPASS)])
            view = gx[:].bitcast(F32).rearrange("p (t g m u) -> p t g m u", t=2, g=NPASS, u=2)
            return lambda: copy_on(eng, view[:, i], bank[:].rearrange("p (g u) m -> p g m u", u=2))

        def x_run(bc, engs):
            gx = grp.tile([P, 4 * NCOL], BF16, name="gx", align_bytes=64)
            evacs = [x_tile(bc, i, gx, engs[i]) for i in range(2)]
            for call in evacs:
                call()
            pending.append(lambda: x_quant(bc, gx, 0, 2))

        def mm(n, b, t):
            acc = accs.tile([P, NCOL], F32, name="acc")
            bc = (b, t // 2)
            for g in range(NPASS):
                nc.tensor.matmul_mx(
                    out=acc[:],
                    lhsT=xq[bc][:, t % 2, g, :].bitcast(FP8X4),
                    lhsT_scale=xs[bc][:, t % 2, g, :],
                    rhs=wq[:, slot(n, g), :].bitcast(FP8X4),
                    rhs_scale=ws[:, slot(n, g), :],
                    start=(g == 0),
                    stop=(g == NPASS - 1),
                )
            return acc

        def store(queue, n, b, tile_, ha, hb):
            h0 = n[1] * HG
            dst = outs[n[0]][b, h0 + ha : h0 + hb].rearrange("h (p t) d -> p h t d", t=TPB)
            queue.dma_start(out=dst.rearrange("p h t d -> p h (t d)"), in_=tile_[:, ha:hb].rearrange("p h t d -> p h (t d)"))

        def rope_mults(acc, t, ab):
            nc.vector.tensor_tensor(
                out=ab[:, :, :, t, :].rearrange("p s h d -> p h s d"),
                in0=acc[:].rearrange("p (h d) -> p h d", d=D).unsqueeze(2).to_broadcast([P, HG, 2, D]),
                in1=tab[:, t].unsqueeze(1).to_broadcast([P, HG, 2, D]),
                op=MUL,
            )

        for i in range(6):
            warm_up()

        gw_first = [grp.tile([P, 1, 4 * NCOL], BF16, name="gw", align_bytes=64) for g in range(NPASS)]
        for rp in range(2):
            banks = [w_bank(Q0, rp, g) for g in range(NPASS)]
            for g in range(NPASS):
                w_evac(banks[g], gw_first[g][:, 0, :], rp, "vs"[g])
        w_quant(slot(Q0, 1), 1, gw_first[1])
        w_quant(slot(Q0, 0), 1, gw_first[0])
        gx_first = grp.tile([P, 4 * NCOL], BF16, name="gx", align_bytes=64)
        for i in range(2):
            evac = x_tile((0, 0), i, gx_first, "s")
            evac()
            x_quant((0, 0), gx_first, i, i + 1)
        x_run((0, 1), "vs")
        x_run((1, 0), "ss")
        x_run((1, 1), "ss")
        for call in pending[0:2]:
            call()
        late = pending[2:]
        pending.clear()

        later_runs = [(n, g) for n in made[1:] for g in range(NPASS)]
        run_step = [2 * j for j in range(len(later_runs))]
        quant_step = [TPB * ((s + TPB + 1) // TPB) for s in run_step]
        copy_units = [(n, b, t) for n in (V0, V1) for b in range(B) for t in range(TPB)]
        rope_units = [(n, b, t) for n in (Q0, K0, Q1, K1) for b in range(B) for t in range(TPB)]
        FIRST_COPY = 10
        acc_of = {}
        gw_of = {}
        held = {}

        for rp in range(2):
            nc.sync.dma_start(out=first[rp][:], in_=w_rows(Q0)[:, 2 * rp : 2 * rp + 2, :])

        for u in range(2):
            acc_of[u] = mm(*rope_units[u])

        for u in range(len(rope_units)):
            n, b, t = rope_units[u]
            if u == 1:
                for call in late:
                    call()
            sharing = [j for j in range(len(later_runs)) if quant_step[j] == u]
            if sharing:
                w_quant(slot(*later_runs[sharing[0]]), len(sharing), gw_of[sharing[0]])
            if u in run_step:
                j = run_step.index(u)
                sharing = [i for i in range(len(later_runs)) if quant_step[i] == quant_step[j]]
                if j == sharing[0]:
                    shared = grp.tile([P, len(sharing), 4 * NCOL], BF16, name="gw", align_bytes=64)
                    for i in sharing:
                        gw_of[i] = shared
                w_run(later_runs[j][0], later_runs[j][1], gw_of[j][:, j - sharing[0], :])
            if FIRST_COPY <= u < FIRST_COPY + len(copy_units):
                cn, cb, ct = copy_units[u - FIRST_COPY]
                if ct == 0:
                    held["v"] = stage.tile([P, HG, TPB, D], F32, name="vv", bufs=2)
                acc_c = mm(cn, cb, ct)
                nc.scalar.copy(out=held["v"][:, :, ct, :], in_=acc_c[:].rearrange("p (h d) -> p h d", d=D))
                if ct == TPB - 1:
                    store(nc.scalar, cn, cb, held["v"], 0, HG)
            if u + 2 < len(rope_units):
                acc_of[u + 2] = mm(*rope_units[u + 2])
            if t == 0:
                held["ab"] = stage.tile([P, 2, HG, TPB, D], F32, name="ab", bufs=4)
            ab = held["ab"]
            rope_mults(acc_of[u], t, ab)
            if t == TPB - 1:
                last = len(rope_units) - 1
                adder = nc.vector if u == last else nc.gpsimd
                pieces = 2 if u >= last - TPB else 1
                for piece in range(pieces):
                    ha = piece * HG // pieces
                    hb = ha + HG // pieces
                    firsts = ab[:, 0, ha:hb].rearrange("p h t (f j) -> p (h t) f j", f=2)
                    seconds = ab[:, 1, ha:hb].rearrange("p h t (f j) -> p (h t) f j", f=2)
                    adder.tensor_tensor(out=firsts, in0=firsts, in1=seconds[:, :, ::-1, :], op=ADD)
                    store(nc.sync, n, b, ab[:, 0], ha, hb)
